import numpy as np
import ml_dtypes


def mxq(x, axis, fmt="e4m3"):
    dtype, down = {"e4m3": (ml_dtypes.float8_e4m3fn, 7), "e5m2": (ml_dtypes.float8_e5m2, 14)}[fmt]
    v = np.moveaxis(np.asarray(x, np.float32).astype(ml_dtypes.bfloat16).astype(np.float64), axis, -1)
    blocks = v.reshape(v.shape[:-1] + (-1, 32))
    amax = np.abs(blocks).max(-1, keepdims=True)
    byte = np.maximum(np.where(amax > 0, np.frexp(amax)[1] - 1 + 127, 0) - down, 1)
    scale = np.exp2(byte - 127.0)
    codes = (blocks / scale).astype(np.float32).astype(dtype).astype(np.float64)
    return np.moveaxis((codes * scale).reshape(v.shape), -1, axis)


WIDE = False


def mx_kscale(k):
    if not WIDE:
        return np.ones(k)
    levels = np.array([10, -10, 5, -5, 0])
    if k % 512:
        return np.exp2(np.random.permutation(np.resize(levels, k // 32))).repeat(32)
    a = np.empty((k // 512, 16))
    for p in range(k // 512):
        a[p, :8] = np.random.permutation(np.resize(levels, 8))
        for g in range(8):
            far = levels[np.abs(levels - a[p, g]) >= 10]
            a[p, g + 8] = far[np.random.randint(len(far))]
    return np.exp2(a.ravel()).repeat(32)


BF16 = ml_dtypes.bfloat16


def bf(x):
    return np.asarray(x, np.float32).astype(BF16)


def f64(x):
    return np.asarray(x).astype(np.float64)


B, T, N, D, H, F = 1, 512, 2, 1024, 8, 1024
S = B * N
EPS = 1e-5


def layernorm(v, g, b):
    mu = v.mean(-1, keepdims=True)
    var = np.square(v - mu).mean(-1, keepdims=True)
    return (v - mu) / np.sqrt(var + EPS) * g + b


def setup_inputs():
    s = mx_kscale(D)
    t = mx_kscale(D)
    return {"ax_cat": bf(np.random.standard_normal((S, T, D)) * 4.0 * s),
            "features": bf(np.random.standard_normal((B, T, N, D))),
            "wout_w": bf(np.random.standard_normal((D, D)) * 0.5 / np.sqrt(D) / s),
            "ln_g": bf((1.0 + 0.1 * np.random.standard_normal(D)) * t),
            "ln_b": bf(0.1 * np.random.standard_normal(D) * t),
            "ff1_w": bf(np.random.standard_normal((F, D)) / np.sqrt(D) / t),
            "ff1_b": bf(0.1 * np.random.standard_normal(F))}


def reference(ax_cat, features, wout_w, ln_g, ln_b, ff1_w, ff1_b):
    x = f64(features).transpose(0, 2, 1, 3).reshape(S, T, D)
    y = mxq(f64(ax_cat), 2, "e4m3") @ mxq(f64(wout_w), 1, "e4m3").T
    m = layernorm(y + x, f64(ln_g), f64(ln_b))
    return np.maximum((mxq(m, 2, "e4m3") @ mxq(f64(ff1_w), 1, "e4m3").T) + f64(ff1_b), 0.0)

@@ -1,0 +1,347 @@
+from contextlib import ExitStack
+
+import concourse.mybir as mybir
+from concourse.masks import make_identity
+
+F32 = mybir.dt.float32
+BF16 = mybir.dt.bfloat16
+U32 = mybir.dt.uint32
+U8 = mybir.dt.uint8
+FP8X4 = mybir.dt.float8_e4m3fn_x4
+ACT = mybir.ActivationFunctionType
+ALU = mybir.AluOpType
+
+P = 128
+PACK = 4
+D = 1024
+PASSES = D // (P * PACK)
+BANK = 512
+HALVES = D // BANK
+ROW_BLOCKS = D // P
+SEQS = 2
+TIME_BLOCKS = 4
+TOKEN_BLOCKS = SEQS * TIME_BLOCKS
+EPS = 1e-5
+
+FLOPS = 2 * 2 * (SEQS * 512) * D * D
+
+
+def tile_temporalatt_pb_kernel(tc, ax_cat, features, wout_w, ln_g, ln_b, ff1_w, ff1_b, out):
+    nc = tc.nc
+
+    ax_view = ax_cat.rearrange("s (b p) k -> p b s k", p=P)
+    x_view = features.rearrange("o (b p) s d -> p (o b) s d", p=P)
+    out_view = out.rearrange("s (b p) f -> p b s f", p=P)
+    wout_view = wout_w.rearrange("(g p t) k -> p g t k", p=P, t=PACK)
+    ff1_view = ff1_w.rearrange("(j p) k -> p j k", p=P)
+
+    with ExitStack() as stack:
+        stack.enter_context(tc.manual_schedule())
+        keep = stack.enter_context(tc.tile_pool(name="keep", bufs=1))
+        stage = stack.enter_context(tc.tile_pool(name="stage", bufs=2))
+        stats = stack.enter_context(tc.tile_pool(name="stats", bufs=4))
+        results = stack.enter_context(tc.tile_pool(name="results", bufs=3))
+        psum_t = stack.enter_context(tc.psum_pool(name="psum_t", bufs=4))
+        psum_mm = stack.enter_context(tc.psum_pool(name="psum_mm", bufs=4))
+
+        ident = keep.tile([P, P], F32)
+        make_identity(nc, ident[:])
+        ones = keep.tile([P, P], BF16)
+        nc.gpsimd.memset(ones[:], 1.0)
+        bias_row = keep.tile([P, D], BF16)
+        nc.gpsimd.memset(bias_row[:], 0.0)
+        ln_rows = keep.tile([P, BANK], BF16)
+        nc.gpsimd.memset(ln_rows[:], 0.0)
+        eps_col = keep.tile([P, 1], F32)
+        nc.vector.memset(eps_col[:], EPS)
+        warm = keep.tile([P, 1], F32)
+        nc.scalar.activation(out=warm[:], in_=eps_col[:], func=ACT.Sqrt)
+
+        nc.scalar.dma_start(out=ln_rows[0:2, :], in_=ln_g.rearrange("(g w) -> g w", g=PASSES))
+        nc.scalar.dma_start(out=ln_rows[2:4, :], in_=ln_b.rearrange("(g w) -> g w", g=PASSES))
+        nc.scalar.dma_start(out=bias_row[0:1, :], in_=ff1_b.rearrange("(o f) -> o f", o=1))
+
+        wout_raw = keep.tile([P, 2, 4, D], BF16)
+        ax_raw = keep.tile([P, TIME_BLOCKS, SEQS, D], BF16)
+        x_raw = keep.tile([P, TIME_BLOCKS, SEQS, D], BF16)
+        ff1_raw = keep.tile([P, ROW_BLOCKS, D], BF16)
+
+        def load_ax(b):
+            nc.sync.dma_start(out=ax_raw[:, b], in_=ax_view[:, b])
+
+        def load_x(b):
+            nc.sync.dma_start(out=x_raw[:, b], in_=x_view[:, b])
+
+        def load_ff1(j):
+            nc.sync.dma_start(out=ff1_raw[:, j : j + 2], in_=ff1_view[:, j : j + 2])
+
+        load_ax(0)
+        for e in range(2):
+            for c in range(0, 4, 2):
+                nc.sync.dma_start(out=wout_raw[:, e, c : c + 2], in_=wout_view[:, e, c : c + 2])
+        load_x(0)
+        load_ax(1)
+        load_ax(2)
+        load_x(1)
+        load_ax(3)
+        load_ff1(0)
+        load_ff1(2)
+        load_x(2)
+        load_ff1(4)
+        load_ff1(6)
+        load_x(3)
+
+        w1_codes = keep.tile([P, HALVES, PASSES, BANK], U32, align_bytes=64)
+        w1_scales = keep.tile([P, HALVES, PASSES, BANK], U8, align_bytes=64)
+        w2_codes = keep.tile([P, HALVES, PASSES, BANK], U32, align_bytes=64)
+        w2_scales = keep.tile([P, HALVES, PASSES, BANK], U8, align_bytes=64)
+        a_codes = keep.tile([P, TOKEN_BLOCKS, PASSES, P], U32, align_bytes=64)
+        a_scales = keep.tile([P, TOKEN_BLOCKS, PASSES, P], U8, align_bytes=64)
+        m_codes = keep.tile([P, TOKEN_BLOCKS, PASSES, P], U32, align_bytes=64)
+        m_scales = keep.tile([P, TOKEN_BLOCKS, PASSES, P], U8, align_bytes=64)
+
+        def turn_rows(raw_rows):
+            words = raw_rows.bitcast(F32)
+            bank = psum_t.tile([P, 4, P], F32, tag="turned")
+            for g in range(PASSES):
+                for u in range(2):
+                    pair = words[:, 2 * P * g + u : 2 * P * (g + 1) : 2]
+                    nc.tensor.transpose(bank[:, 2 * g + u, :], pair, ident[:])
+            return bank
+
+        def group_rows(copy, bank, grouped_rows):
+            copy(out=grouped_rows.bitcast(F32), in_=bank[:].rearrange("p (g u) r -> p g r u", u=2))
+
+        def quantise(grouped, codes, scales):
+            nc.vector.quantize_mx(
+                out=codes.rearrange("p g r -> p (g r)").bitcast(FP8X4),
+                scales=scales.rearrange("p g r -> p (g r)"),
+                in_=grouped.rearrange("p g r t -> p (g r t)"),
+            )
+
+        def matmul_group(lhs_codes, lhs_scales, rhs_codes, rhs_scales):
+            acc = psum_mm.tile([P, BANK], F32, tag="acc")
+            for g in range(PASSES):
+                nc.tensor.matmul_mx(
+                    out=acc[:],
+                    lhsT=lhs_codes[:, g, :].bitcast(FP8X4),
+                    lhsT_scale=lhs_scales[:, g, :],
+                    rhs=rhs_codes[:, g, :].bitcast(FP8X4),
+                    rhs_scale=rhs_scales[:, g, :],
+                    start=(g == 0),
+                    stop=(g == PASSES - 1),
+                )
+            return acc
+
+        def prepare_tokens(b, copies):
+            a_grouped = stage.tile([P, SEQS * PASSES, P, PACK], BF16, align_bytes=64, tag="a_grouped", bufs=3)
+            for s in range(SEQS):
+                bank = turn_rows(ax_raw[:, b, s, :])
+                group_rows(copies[s], bank, a_grouped[:, s * PASSES : (s + 1) * PASSES])
+            return a_grouped
+
+        def quantise_tokens(b, a_grouped):
+            first = SEQS * b
+            nc.vector.quantize_mx(
+                out=a_codes[:, first : first + SEQS].rearrange("p i g r -> p (i g r)").bitcast(FP8X4),
+                scales=a_scales[:, first : first + SEQS].rearrange("p i g r -> p (i g r)"),
+                in_=a_grouped[:].rearrange("p g r t -> p (g r t)"),
+            )
+
+        def prepare_weight_rows(raw_rows, copy, w_grouped, c):
+            group_rows(copy, turn_rows(raw_rows), w_grouped[:, :, c * P : (c + 1) * P, :])
+
+        def new_w_grouped():
+            w_grouped = stage.tile([P, PASSES, BANK, PACK], BF16, align_bytes=64, tag="w_grouped")
+            return w_grouped
+
+        y_banks = {}
+        r_tiles = {}
+        neg_means = {}
+        stds = {}
+        z_tiles = {}
+        zt_banks = {}
+        plane_tiles = {}
+        m_groupeds = {}
+        o_banks = {}
+
+        def project(i):
+            y_banks[i] = [
+                matmul_group(a_codes[:, i], a_scales[:, i], w1_codes[:, e], w1_scales[:, e])
+                for e in range(HALVES)
+            ]
+
+        def add_residual(i):
+            b, s = divmod(i, SEQS)
+            r = stage.tile([P, D], F32, tag="r", bufs=4)
+            sums = stats.tile([P, HALVES], F32, tag="sums")
+            x_ordered = x_raw[:, b, s, :].rearrange("p (g q t) -> p g t q", g=PASSES, t=PACK)
+            for e in range(HALVES):
+                nc.vector.scalar_tensor_tensor(
+                    out=r[:, e * BANK : (e + 1) * BANK].rearrange("p (t q) -> p t q", t=PACK),
+                    in0=y_banks[i][e][:].rearrange("p (t q) -> p t q", t=PACK),
+                    scalar=1.0,
+                    in1=x_ordered[:, e],
+                    op0=ALU.mult,
+                    op1=ALU.add,
+                    accum_out=sums[:, e : e + 1],
+                )
+            r_tiles[i] = r
+            return sums
+
+        def deviation(i, sums):
+            scaled = stats.tile([P, HALVES], F32, tag="scaled")
+            neg_mean = stats.tile([P, 1], F32, tag="neg_mean")
+            nc.scalar.activation(
+                out=scaled[:], in_=sums[:], func=ACT.Identity, scale=-1.0 / D, accum_out=neg_mean[:]
+            )
+            squares = stage.tile([P, D], BF16, tag="squares")
+            sum_sq = stats.tile([P, 1], F32, tag="sum_sq")
+            nc.scalar.activation(
+                out=squares[:], in_=r_tiles[i][:], func=ACT.Square, bias=neg_mean[:], accum_out=sum_sq[:]
+            )
+            std = stats.tile([P, 1], F32, tag="std")
+            nc.scalar.activation(out=std[:], in_=sum_sq[:], func=ACT.Sqrt, scale=1.0 / D, bias=eps_col[:])
+            neg_means[i] = neg_mean
+            stds[i] = std
+
+        def normalise(i):
+            inv_std = stats.tile([P, 1], F32, tag="inv_std")
+            nc.vector.reciprocal(out=inv_std[:], in_=stds[i][:])
+            z = stage.tile([P, D], F32, tag="z", bufs=3)
+            nc.gpsimd.tensor_scalar(
+                out=z[:],
+                in0=r_tiles[i][:],
+                scalar1=neg_means[i][:],
+                scalar2=inv_std[:],
+                op0=ALU.add,
+                op1=ALU.mult,
+            )
+            z_tiles[i] = z
+
+        def turn_normed(i):
+            zt_banks[i] = []
+            for g in range(PASSES):
+                bank = psum_t.tile([P, PACK, P], F32, tag="turned")
+                for t in range(PACK):
+                    first = g * BANK + t * P
+                    nc.tensor.transpose(bank[:, t, :], z_tiles[i][:, first : first + P], ident[:])
+                zt_banks[i].append(bank)
+
+        def affine(i):
+            planes = stage.tile([P, PASSES, PACK, P], BF16, tag="planes")
+            for g in range(PASSES):
+                for t in range(PACK):
+                    j = PACK * g + t
+                    nc.scalar.activation(
+                        out=planes[:, g, t, :],
+                        in_=zt_banks[i][g][:, t, :],
+                        func=ACT.Identity,
+                        scale=gain_shift[:, j : j + 1],
+                        bias=gain_shift[:, ROW_BLOCKS + j : ROW_BLOCKS + j + 1],
+                    )
+            plane_tiles[i] = planes
+
+        def group_normed(i):
+            m_grouped = stage.tile([P, PASSES, P, PACK], BF16, align_bytes=64, tag="m_grouped")
+            nc.vector.tensor_copy(out=m_grouped[:], in_=plane_tiles[i][:].rearrange("p g t r -> p g r t"))
+            m_groupeds[i] = m_grouped
+
+        def quantise_normed(i):
+            quantise(m_groupeds[i][:], m_codes[:, i], m_scales[:, i])
+
+        def feed_forward(i):
+            o_banks[i] = [
+                matmul_group(m_codes[:, i], m_scales[:, i], w2_codes[:, h], w2_scales[:, h])
+                for h in range(HALVES)
+            ]
+
+        def finish(i):
+            b, s = divmod(i, SEQS)
+            result = results.tile([P, D], F32, tag="result")
+            for h in range(HALVES):
+                cols = slice(h * BANK, (h + 1) * BANK)
+                nc.vector.tensor_tensor(out=result[:, cols], in0=o_banks[i][h][:], in1=bias_all[:, cols], op=ALU.add)
+                nc.scalar.activation(out=result[:, cols], in_=result[:, cols], func=ACT.Relu)
+                nc.sync.dma_start(out=out_view[:, b, s, cols], in_=result[:, cols])
+
+        both = [nc.scalar.copy, nc.vector.tensor_copy]
+        a_grouped_0 = prepare_tokens(0, both)
+        for e in range(HALVES):
+            w1_grouped = new_w_grouped()
+            for c in range(4):
+                prepare_weight_rows(wout_raw[:, e, c, :], both[c % 2], w1_grouped, c)
+            if e == 0:
+                quantise_tokens(0, a_grouped_0)
+            quantise(w1_grouped[:], w1_codes[:, e], w1_scales[:, e])
+
+        ln_words = ln_rows[:].bitcast(F32)
+        ln_bank = psum_t.tile([P, 4, P], F32, tag="turned")
+        for u in range(2):
+            nc.tensor.transpose(ln_bank[:, u, :], ln_words[:, u : 2 * P : 2], ident[:])
+        gain_shift = keep.tile([P, 2 * ROW_BLOCKS], F32)
+        nc.vector.tensor_copy(
+            out=gain_shift[:].rearrange("p (r u e) -> p u r e", u=2, e=2),
+            in_=ln_bank[:, 0:2, 0:4].bitcast(BF16).rearrange("p u (r e) -> p u r e", e=2),
+        )
+
+        bias_all = keep.tile([P, D], F32)
+        for h in range(HALVES):
+            cols = slice(h * BANK, (h + 1) * BANK)
+            bias_bank = psum_mm.tile([P, BANK], F32, tag="acc")
+            nc.tensor.matmul(out=bias_bank[:], lhsT=ones[:], rhs=bias_row[:, cols], start=True, stop=True)
+            nc.scalar.copy(out=bias_all[:, cols], in_=bias_bank[:])
+
+        CHUNKS = (TIME_BLOCKS - 1) + ROW_BLOCKS // 2
+        grouped_chunks = {}
+
+        def prepare_chunk(k):
+            if k < TIME_BLOCKS - 1:
+                grouped_chunks[k] = prepare_tokens(k + 1, [nc.scalar.copy, nc.scalar.copy])
+            else:
+                h, first = divmod(2 * (k - (TIME_BLOCKS - 1)), 4)
+                if first == 0:
+                    grouped_chunks[k] = new_w_grouped()
+                else:
+                    grouped_chunks[k] = grouped_chunks[k - 1]
+                for c in (first, first + 1):
+                    prepare_weight_rows(ff1_raw[:, 4 * h + c, :], nc.scalar.copy, grouped_chunks[k], c)
+
+        def quantise_chunk(k):
+            if k < TIME_BLOCKS - 1:
+                quantise_tokens(k + 1, grouped_chunks[k])
+            else:
+                h, first = divmod(2 * (k - (TIME_BLOCKS - 1)), 4)
+                if first == 2:
+                    quantise(grouped_chunks[k][:], w2_codes[:, h], w2_scales[:, h])
+
+        RESIDUAL, NORMALISE, TURN, AFFINE, GROUP, FEED_FORWARD, FINISH = 1, 3, 4, 5, 6, 7, 8
+
+        def live(i):
+            return 0 <= i < TOKEN_BLOCKS
+
+        for n in range(TOKEN_BLOCKS + FINISH):
+            for k in range(CHUNKS):
+                if max(0, k - 1) == n:
+                    prepare_chunk(k)
+            if live(n - NORMALISE):
+                normalise(n - NORMALISE)
+            if live(n - TURN):
+                turn_normed(n - TURN)
+            if live(n - AFFINE):
+                affine(n - AFFINE)
+            if live(n - RESIDUAL):
+                deviation(n - RESIDUAL, add_residual(n - RESIDUAL))
+            for k in range(CHUNKS):
+                if max(0, k - 1) + 1 == n:
+                    quantise_chunk(k)
+            if live(n - GROUP):
+                group_normed(n - GROUP)
+            if live(n - FINISH):
+                finish(n - FINISH)
+            if live(n - GROUP):
+                quantise_normed(n - GROUP)
+            if live(n):
+                project(n)
+            if live(n - FEED_FORWARD):
+                feed_forward(n - FEED_FORWARD)

@@ -75,21 +75,30 @@ def tile_temporalatt_pb_kernel(tc, ax_cat, features, wout_w, ln_g, ln_b, ff1_w, 
         def load_ff1(j):
             nc.sync.dma_start(out=ff1_raw[:, j : j + 2], in_=ff1_view[:, j : j + 2])
 
-        load_ax(0)
-        for e in range(2):
-            for c in range(0, 4, 2):
-                nc.sync.dma_start(out=wout_raw[:, e, c : c + 2], in_=wout_view[:, e, c : c + 2])
-        load_x(0)
+        def load_wout(g, t):
+            nc.sync.dma_start(out=wout_raw[:, g, t : t + 2], in_=wout_view[:, g, t : t + 2])
+
+        def load_ax_block(i):
+            b, s = divmod(i, SEQS)
+            nc.sync.dma_start(out=ax_raw[:, b, s], in_=ax_view[:, b, s])
+
+        load_ax_block(0)
+        load_wout(1, 0)
+        load_wout(0, 2)
+        load_wout(0, 0)
+        load_ax_block(1)
+        load_wout(1, 2)
         load_ax(1)
-        load_ax(2)
-        load_x(1)
-        load_ax(3)
-        load_ff1(0)
         load_ff1(2)
-        load_x(2)
-        load_ff1(4)
+        load_ff1(0)
         load_ff1(6)
+        load_ff1(4)
+        load_x(0)
+        load_ax(2)
         load_x(3)
+        load_x(2)
+        load_ax(3)
+        load_x(1)
 
         w1_codes = keep.tile([P, HALVES, PASSES, BANK], U32, align_bytes=64)
         w1_scales = keep.tile([P, HALVES, PASSES, BANK], U8, align_bytes=64)
@@ -133,30 +142,13 @@ def tile_temporalatt_pb_kernel(tc, ax_cat, features, wout_w, ln_g, ln_b, ff1_w, 
                 )
             return acc
 
-        def prepare_tokens(b, copies):
-            a_grouped = stage.tile([P, SEQS * PASSES, P, PACK], BF16, align_bytes=64, tag="a_grouped", bufs=3)
-            for s in range(SEQS):
-                bank = turn_rows(ax_raw[:, b, s, :])
-                group_rows(copies[s], bank, a_grouped[:, s * PASSES : (s + 1) * PASSES])
-            return a_grouped
+        on_scalar, on_vector = nc.scalar.copy, nc.vector.tensor_copy
 
-        def quantise_tokens(b, a_grouped):
-            first = SEQS * b
-            nc.vector.quantize_mx(
-                out=a_codes[:, first : first + SEQS].rearrange("p i g r -> p (i g r)").bitcast(FP8X4),
-                scales=a_scales[:, first : first + SEQS].rearrange("p i g r -> p (i g r)"),
-                in_=a_grouped[:].rearrange("p g r t -> p (g r t)"),
-            )
-
-        def prepare_weight_rows(raw_rows, copy, w_grouped, c):
-            group_rows(copy, turn_rows(raw_rows), w_grouped[:, :, c * P : (c + 1) * P, :])
-
-        def new_w_grouped():
-            w_grouped = stage.tile([P, PASSES, BANK, PACK], BF16, align_bytes=64, tag="w_grouped")
-            return w_grouped
-
+        a_groupeds = {}
+        w2_groupeds = {}
         y_banks = {}
         r_tiles = {}
+        row_sums = {}
         neg_means = {}
         stds = {}
         z_tiles = {}
@@ -164,36 +156,63 @@ def tile_temporalatt_pb_kernel(tc, ax_cat, features, wout_w, ln_g, ln_b, ff1_w, 
         plane_tiles = {}
         m_groupeds = {}
         o_banks = {}
+        results_of = {}
+        banks = {}
 
-        def project(i):
-            y_banks[i] = [
-                matmul_group(a_codes[:, i], a_scales[:, i], w1_codes[:, e], w1_scales[:, e])
-                for e in range(HALVES)
-            ]
-
-        def add_residual(i):
+        def turn_tokens(i):
             b, s = divmod(i, SEQS)
-            r = stage.tile([P, D], F32, tag="r", bufs=4)
-            sums = stats.tile([P, HALVES], F32, tag="sums")
+            banks["a", i] = turn_rows(ax_raw[:, b, s, :])
+
+        def group_tokens(i, copy):
+            a_grouped = stage.tile([P, PASSES, P, PACK], BF16, align_bytes=64, tag="a_grouped", bufs=3)
+            group_rows(copy, banks["a", i], a_grouped[:])
+            a_groupeds[i] = a_grouped
+
+        def quantise_tokens(i):
+            quantise(a_groupeds[i][:], a_codes[:, i], a_scales[:, i])
+
+        def new_w_grouped():
+            w_grouped = stage.tile([P, PASSES, BANK, PACK], BF16, align_bytes=64, tag="w_grouped")
+            return w_grouped
+
+        def turn_ff1(j):
+            banks["w", j] = turn_rows(ff1_raw[:, j, :])
+
+        def group_ff1(j, copy):
+            h, c = divmod(j, 4)
+            if c == 0:
+                w2_groupeds[h] = new_w_grouped()
+            group_rows(copy, banks["w", j], w2_groupeds[h][:, :, c * P : (c + 1) * P, :])
+
+        def quantise_ff1(h):
+            quantise(w2_groupeds[h][:], w2_codes[:, h], w2_scales[:, h])
+
+        def project(i, e):
+            y_banks[i, e] = matmul_group(a_codes[:, i], a_scales[:, i], w1_codes[:, e], w1_scales[:, e])
+
+        def add_residual(i, e):
+            b, s = divmod(i, SEQS)
+            if e == 0:
+                r_tiles[i] = stage.tile([P, D], F32, tag="r", bufs=6, name="r")
+                row_sums[i] = stats.tile([P, HALVES], F32, tag="sums", name="sums")
+            r, sums = r_tiles[i], row_sums[i]
             x_ordered = x_raw[:, b, s, :].rearrange("p (g q t) -> p g t q", g=PASSES, t=PACK)
-            for e in range(HALVES):
+            if True:
                 nc.vector.scalar_tensor_tensor(
                     out=r[:, e * BANK : (e + 1) * BANK].rearrange("p (t q) -> p t q", t=PACK),
-                    in0=y_banks[i][e][:].rearrange("p (t q) -> p t q", t=PACK),
+                    in0=y_banks[i, e][:].rearrange("p (t q) -> p t q", t=PACK),
                     scalar=1.0,
                     in1=x_ordered[:, e],
                     op0=ALU.mult,
                     op1=ALU.add,
                     accum_out=sums[:, e : e + 1],
                 )
-            r_tiles[i] = r
-            return sums
 
-        def deviation(i, sums):
+        def deviation(i):
             scaled = stats.tile([P, HALVES], F32, tag="scaled")
             neg_mean = stats.tile([P, 1], F32, tag="neg_mean")
             nc.scalar.activation(
-                out=scaled[:], in_=sums[:], func=ACT.Identity, scale=-1.0 / D, accum_out=neg_mean[:]
+                out=scaled[:], in_=row_sums[i][:], func=ACT.Identity, scale=-1.0 / D, accum_out=neg_mean[:]
             )
             squares = stage.tile([P, D], BF16, tag="squares")
             sum_sq = stats.tile([P, 1], F32, tag="sum_sq")
@@ -205,11 +224,11 @@ def tile_temporalatt_pb_kernel(tc, ax_cat, features, wout_w, ln_g, ln_b, ff1_w, 
             neg_means[i] = neg_mean
             stds[i] = std
 
-        def normalise(i):
+        def normalise(i, engine):
             inv_std = stats.tile([P, 1], F32, tag="inv_std")
             nc.vector.reciprocal(out=inv_std[:], in_=stds[i][:])
             z = stage.tile([P, D], F32, tag="z", bufs=3)
-            nc.gpsimd.tensor_scalar(
+            engine.tensor_scalar(
                 out=z[:],
                 in0=r_tiles[i][:],
                 scalar1=neg_means[i][:],
@@ -219,129 +238,150 @@ def tile_temporalatt_pb_kernel(tc, ax_cat, features, wout_w, ln_g, ln_b, ff1_w, 
             )
             z_tiles[i] = z
 
-        def turn_normed(i):
-            zt_banks[i] = []
-            for g in range(PASSES):
+        def turn_normed(i, g):
+            if True:
                 bank = psum_t.tile([P, PACK, P], F32, tag="turned")
                 for t in range(PACK):
                     first = g * BANK + t * P
                     nc.tensor.transpose(bank[:, t, :], z_tiles[i][:, first : first + P], ident[:])
-                zt_banks[i].append(bank)
+                zt_banks[i, g] = bank
 
-        def affine(i):
-            planes = stage.tile([P, PASSES, PACK, P], BF16, tag="planes")
-            for g in range(PASSES):
-                for t in range(PACK):
-                    j = PACK * g + t
+        def affine(i, g, engine):
+            if (i,) not in plane_tiles:
+                plane_tiles[i,] = stage.tile([P, PASSES, PACK, P], BF16, tag="planes", bufs=2, name="planes")
+            planes = plane_tiles[i,]
+            for t in range(PACK):
+                j = PACK * g + t
+                if engine == "V" or (engine == "M" and t % 2):
+                    nc.vector.tensor_scalar(out=planes[:, g, t, :], in0=zt_banks[i, g][:, t, :], scalar1=gain_shift[:, j : j + 1],
+                        scalar2=gain_shift[:, ROW_BLOCKS + j : ROW_BLOCKS + j + 1], op0=ALU.mult, op1=ALU.add)
+                else:
                     nc.scalar.activation(
                         out=planes[:, g, t, :],
-                        in_=zt_banks[i][g][:, t, :],
+                        in_=zt_banks[i, g][:, t, :],
                         func=ACT.Identity,
                         scale=gain_shift[:, j : j + 1],
                         bias=gain_shift[:, ROW_BLOCKS + j : ROW_BLOCKS + j + 1],
                     )
-            plane_tiles[i] = planes
 
-        def group_normed(i):
-            m_grouped = stage.tile([P, PASSES, P, PACK], BF16, align_bytes=64, tag="m_grouped")
-            nc.vector.tensor_copy(out=m_grouped[:], in_=plane_tiles[i][:].rearrange("p g t r -> p g r t"))
-            m_groupeds[i] = m_grouped
+        def group_normed(i, g, engine):
+            if i not in m_groupeds:
+                m_groupeds[i] = stage.tile(
+                    [P, PASSES, P, PACK], BF16, align_bytes=64, tag="m_grouped", bufs=2, name="m_grouped"
+                )
+            out, in_ = m_groupeds[i][:, g], plane_tiles[i,][:, g].rearrange("p t r -> p r t")
+            if engine is nc.gpsimd:
+                engine.tensor_scalar(out=out, in0=in_, scalar1=1.0, scalar2=0.0, op0=ALU.mult, op1=ALU.add)
+            else:
+                engine.tensor_copy(out=out, in_=in_)
 
         def quantise_normed(i):
             quantise(m_groupeds[i][:], m_codes[:, i], m_scales[:, i])
 
-        def feed_forward(i):
-            o_banks[i] = [
-                matmul_group(m_codes[:, i], m_scales[:, i], w2_codes[:, h], w2_scales[:, h])
-                for h in range(HALVES)
-            ]
+        def feed_forward(i, h):
+            o_banks[i, h] = matmul_group(m_codes[:, i], m_scales[:, i], w2_codes[:, h], w2_scales[:, h])
 
-        def finish(i):
+        def add_bias(i, h):
+            if i not in results_of:
+                results_of[i] = results.tile([P, D], F32, tag="result", name="result")
+            cols = slice(h * BANK, (h + 1) * BANK)
+            nc.vector.tensor_tensor(
+                out=results_of[i][:, cols], in0=o_banks[i, h][:], in1=bias_all[:, cols], op=ALU.add
+            )
+
+        def rectify(i, h, eng):
             b, s = divmod(i, SEQS)
-            result = results.tile([P, D], F32, tag="result")
+            cols = slice(h * BANK, (h + 1) * BANK)
+            part = results_of[i][:, cols]
+            if eng == "V":
+                nc.vector.tensor_scalar_max(part, part, 0.0)
+            elif eng == "G":
+                nc.gpsimd.tensor_scalar(out=part, in0=part, scalar1=0.0, scalar2=0.0, op0=ALU.max, op1=ALU.add)
+            else:
+                nc.scalar.activation(out=part, in_=part, func=ACT.Relu)
+            nc.sync.dma_start(out=out_view[:, b, s, cols], in_=part)
+
+        def w1_block(e, c, eng):
+            if e not in w1_groupeds:
+                w1_groupeds[e] = new_w_grouped()
+            banks["w1", e, c] = turn_rows(wout_raw[:, e, c, :])
+            group_rows(on_scalar if eng == "S" else on_vector, banks["w1", e, c], w1_groupeds[e][:, :, c * P : (c + 1) * P, :])
+
+        w1_groupeds = {}
+
+        gain_shift = keep.tile([P, 2 * ROW_BLOCKS], F32)
+        bias_all = keep.tile([P, D], F32)
+
+        def spread_ln():
+            ln_words = ln_rows[:].bitcast(F32)
+            ln_bank = psum_t.tile([P, 4, P], F32, tag="turned")
+            for u in range(2):
+                nc.tensor.transpose(ln_bank[:, u, :], ln_words[:, u : 2 * P : 2], ident[:])
+            nc.vector.tensor_copy(
+                out=gain_shift[:].rearrange("p (r u e) -> p u r e", u=2, e=2),
+                in_=ln_bank[:, 0:2, 0:4].bitcast(BF16).rearrange("p u (r e) -> p u r e", e=2),
+            )
+
+        def spread_bias():
             for h in range(HALVES):
                 cols = slice(h * BANK, (h + 1) * BANK)
-                nc.vector.tensor_tensor(out=result[:, cols], in0=o_banks[i][h][:], in1=bias_all[:, cols], op=ALU.add)
-                nc.scalar.activation(out=result[:, cols], in_=result[:, cols], func=ACT.Relu)
-                nc.sync.dma_start(out=out_view[:, b, s, cols], in_=result[:, cols])
+                bias_bank = psum_mm.tile([P, BANK], F32, tag="acc")
+                nc.tensor.matmul(out=bias_bank[:], lhsT=ones[:], rhs=bias_row[:, cols], start=True, stop=True)
+                nc.scalar.copy(out=bias_all[:, cols], in_=bias_bank[:])
 
-        both = [nc.scalar.copy, nc.vector.tensor_copy]
-        a_grouped_0 = prepare_tokens(0, both)
-        for e in range(HALVES):
-            w1_grouped = new_w_grouped()
-            for c in range(4):
-                prepare_weight_rows(wout_raw[:, e, c, :], both[c % 2], w1_grouped, c)
-            if e == 0:
-                quantise_tokens(0, a_grouped_0)
-            quantise(w1_grouped[:], w1_codes[:, e], w1_scales[:, e])
+        turn_tokens(0)
+        w1_block(1, 0, "S")
+        w1_block(1, 1, "V")
+        w1_block(0, 3, "V")
+        w1_block(0, 2, "S")
+        w1_block(0, 0, "S")
+        w1_block(0, 1, "V")
+        group_tokens(0, on_scalar)
+        quantise_tokens(0)
+        w1_block(1, 3, "V")
+        w1_block(1, 2, "S")
+        quantise(w1_groupeds[1][:], w1_codes[:, 1], w1_scales[:, 1])
+        quantise(w1_groupeds[0][:], w1_codes[:, 0], w1_scales[:, 0])
 
-        ln_words = ln_rows[:].bitcast(F32)
-        ln_bank = psum_t.tile([P, 4, P], F32, tag="turned")
-        for u in range(2):
-            nc.tensor.transpose(ln_bank[:, u, :], ln_words[:, u : 2 * P : 2], ident[:])
-        gain_shift = keep.tile([P, 2 * ROW_BLOCKS], F32)
-        nc.vector.tensor_copy(
-            out=gain_shift[:].rearrange("p (r u e) -> p u r e", u=2, e=2),
-            in_=ln_bank[:, 0:2, 0:4].bitcast(BF16).rearrange("p u (r e) -> p u r e", e=2),
-        )
+        def step(i, piece, *how):
+            if 0 <= i < TOKEN_BLOCKS:
+                piece(i, *how)
 
-        bias_all = keep.tile([P, D], F32)
-        for h in range(HALVES):
-            cols = slice(h * BANK, (h + 1) * BANK)
-            bias_bank = psum_mm.tile([P, BANK], F32, tag="acc")
-            nc.tensor.matmul(out=bias_bank[:], lhsT=ones[:], rhs=bias_row[:, cols], start=True, stop=True)
-            nc.scalar.copy(out=bias_all[:, cols], in_=bias_bank[:])
-
-        CHUNKS = (TIME_BLOCKS - 1) + ROW_BLOCKS // 2
-        grouped_chunks = {}
-
-        def prepare_chunk(k):
-            if k < TIME_BLOCKS - 1:
-                grouped_chunks[k] = prepare_tokens(k + 1, [nc.scalar.copy, nc.scalar.copy])
-            else:
-                h, first = divmod(2 * (k - (TIME_BLOCKS - 1)), 4)
-                if first == 0:
-                    grouped_chunks[k] = new_w_grouped()
-                else:
-                    grouped_chunks[k] = grouped_chunks[k - 1]
-                for c in (first, first + 1):
-                    prepare_weight_rows(ff1_raw[:, 4 * h + c, :], nc.scalar.copy, grouped_chunks[k], c)
-
-        def quantise_chunk(k):
-            if k < TIME_BLOCKS - 1:
-                quantise_tokens(k + 1, grouped_chunks[k])
-            else:
-                h, first = divmod(2 * (k - (TIME_BLOCKS - 1)), 4)
-                if first == 2:
-                    quantise(grouped_chunks[k][:], w2_codes[:, h], w2_scales[:, h])
-
-        RESIDUAL, NORMALISE, TURN, AFFINE, GROUP, FEED_FORWARD, FINISH = 1, 3, 4, 5, 6, 7, 8
-
-        def live(i):
-            return 0 <= i < TOKEN_BLOCKS
-
-        for n in range(TOKEN_BLOCKS + FINISH):
-            for k in range(CHUNKS):
-                if max(0, k - 1) == n:
-                    prepare_chunk(k)
-            if live(n - NORMALISE):
-                normalise(n - NORMALISE)
-            if live(n - TURN):
-                turn_normed(n - TURN)
-            if live(n - AFFINE):
-                affine(n - AFFINE)
-            if live(n - RESIDUAL):
-                deviation(n - RESIDUAL, add_residual(n - RESIDUAL))
-            for k in range(CHUNKS):
-                if max(0, k - 1) + 1 == n:
-                    quantise_chunk(k)
-            if live(n - GROUP):
-                group_normed(n - GROUP)
-            if live(n - FINISH):
-                finish(n - FINISH)
-            if live(n - GROUP):
-                quantise_normed(n - GROUP)
-            if live(n):
-                project(n)
-            if live(n - FEED_FORWARD):
-                feed_forward(n - FEED_FORWARD)
+        for n in range(-3, 16):
+            step(n - 5, turn_normed, 1)
+            step(n - 1, add_residual, 0)
+            step(n - 2, deviation)
+            step(n - 4, turn_normed, 0)
+            step(n - 8, add_bias, 1)
+            step(n - 7, feed_forward, 0)
+            step(n - 5, affine, 1, "S")
+            step(n - 1, add_residual, 1)
+            step(n - 6, group_normed, 1, nc.vector)
+            step(n - 8, rectify, 0, "S")
+            if n == 3:
+                spread_bias()
+            step(n - 8, rectify, 1, "V")
+            if n + 3 >= 1:
+                step(n + 3, turn_tokens)
+            step(n - 6, quantise_normed)
+            if n + 1 >= 1:
+                step(n + 1, quantise_tokens)
+            if n == 1:
+                spread_ln()
+            step(n - 5, group_normed, 0, nc.vector)
+            for j in range(max(0, 8 * (n)), min(8, 8 * (n + 1))):
+                turn_ff1(j)
+            for j in range(max(0, 8 * (n)), min(8, 8 * (n + 1))):
+                group_ff1(j, on_scalar)
+            step(n - 4, affine, 0, "S")
+            if n + 3 >= 1:
+                step(n + 3, group_tokens, on_scalar)
+            step(n, project, 0)
+            if n == 0:
+                quantise_ff1(0)
+            if n == 3:
+                quantise_ff1(1)
+            step(n - 7, feed_forward, 1)
+            step(n, project, 1)
+            step(n - 2, normalise, nc.gpsimd)
+            step(n - 7, add_bias, 0)

@@ -46,10 +46,7 @@ def tile_temporalatt_pb_kernel(tc, ax_cat, features, wout_w, ln_g, ln_b, ff1_w, 
 
         ident = keep.tile([P, P], F32)
         make_identity(nc, ident[:])
-        ones = keep.tile([P, P], BF16)
-        nc.gpsimd.memset(ones[:], 1.0)
-        bias_row = keep.tile([P, D], BF16)
-        nc.gpsimd.memset(bias_row[:], 0.0)
+        bias_all = keep.tile([P, D], BF16)
         ln_rows = keep.tile([P, BANK], BF16)
         nc.gpsimd.memset(ln_rows[:], 0.0)
         eps_col = keep.tile([P, 1], F32)
@@ -59,7 +56,6 @@ def tile_temporalatt_pb_kernel(tc, ax_cat, features, wout_w, ln_g, ln_b, ff1_w, 
 
         nc.scalar.dma_start(out=ln_rows[0:2, :], in_=ln_g.rearrange("(g w) -> g w", g=PASSES))
         nc.scalar.dma_start(out=ln_rows[2:4, :], in_=ln_b.rearrange("(g w) -> g w", g=PASSES))
-        nc.scalar.dma_start(out=bias_row[0:1, :], in_=ff1_b.rearrange("(o f) -> o f", o=1))
 
         wout_raw = keep.tile([P, 2, 4, D], BF16)
         ax_raw = keep.tile([P, TIME_BLOCKS, SEQS, D], BF16)
@@ -82,23 +78,24 @@ def tile_temporalatt_pb_kernel(tc, ax_cat, features, wout_w, ln_g, ln_b, ff1_w, 
             b, s = divmod(i, SEQS)
             nc.sync.dma_start(out=ax_raw[:, b, s], in_=ax_view[:, b, s])
 
+        load_wout(0, 0)
+        load_wout(0, 2)
         load_ax_block(0)
         load_wout(1, 0)
-        load_wout(0, 2)
-        load_wout(0, 0)
-        load_ax_block(1)
         load_wout(1, 2)
+        load_ax_block(1)
         load_ax(1)
-        load_ff1(2)
-        load_ff1(0)
-        load_ff1(6)
-        load_ff1(4)
         load_x(0)
         load_ax(2)
-        load_x(3)
-        load_x(2)
-        load_ax(3)
         load_x(1)
+        load_ax(3)
+        load_ff1(0)
+        load_ff1(2)
+        load_x(2)
+        load_ff1(4)
+        load_ff1(6)
+        load_x(3)
+        nc.sync.dma_start(out=bias_all[:], in_=ff1_b.partition_broadcast(P))
 
         w1_codes = keep.tile([P, HALVES, PASSES, BANK], U32, align_bytes=64)
         w1_scales = keep.tile([P, HALVES, PASSES, BANK], U8, align_bytes=64)
@@ -310,7 +307,6 @@ def tile_temporalatt_pb_kernel(tc, ax_cat, features, wout_w, ln_g, ln_b, ff1_w, 
         w1_groupeds = {}
 
         gain_shift = keep.tile([P, 2 * ROW_BLOCKS], F32)
-        bias_all = keep.tile([P, D], F32)
 
         def spread_ln():
             ln_words = ln_rows[:].bitcast(F32)
@@ -322,66 +318,57 @@ def tile_temporalatt_pb_kernel(tc, ax_cat, features, wout_w, ln_g, ln_b, ff1_w, 
                 in_=ln_bank[:, 0:2, 0:4].bitcast(BF16).rearrange("p u (r e) -> p u r e", e=2),
             )
 
-        def spread_bias():
-            for h in range(HALVES):
-                cols = slice(h * BANK, (h + 1) * BANK)
-                bias_bank = psum_mm.tile([P, BANK], F32, tag="acc")
-                nc.tensor.matmul(out=bias_bank[:], lhsT=ones[:], rhs=bias_row[:, cols], start=True, stop=True)
-                nc.scalar.copy(out=bias_all[:, cols], in_=bias_bank[:])
-
-        turn_tokens(0)
-        w1_block(1, 0, "S")
-        w1_block(1, 1, "V")
-        w1_block(0, 3, "V")
-        w1_block(0, 2, "S")
         w1_block(0, 0, "S")
         w1_block(0, 1, "V")
+        w1_block(0, 3, "V")
+        turn_tokens(0)
         group_tokens(0, on_scalar)
+        w1_block(0, 2, "S")
         quantise_tokens(0)
+        w1_block(1, 0, "S")
+        quantise(w1_groupeds[0][:], w1_codes[:, 0], w1_scales[:, 0])
+        w1_block(1, 1, "V")
         w1_block(1, 3, "V")
         w1_block(1, 2, "S")
         quantise(w1_groupeds[1][:], w1_codes[:, 1], w1_scales[:, 1])
-        quantise(w1_groupeds[0][:], w1_codes[:, 0], w1_scales[:, 0])
 
         def step(i, piece, *how):
             if 0 <= i < TOKEN_BLOCKS:
                 piece(i, *how)
 
-        for n in range(-3, 16):
-            step(n - 5, turn_normed, 1)
-            step(n - 1, add_residual, 0)
+        for n in range(-4, 16):
+            step(n - 8, add_bias, 0)
+            step(n - 5, affine, 0, "M")
             step(n - 2, deviation)
-            step(n - 4, turn_normed, 0)
-            step(n - 8, add_bias, 1)
-            step(n - 7, feed_forward, 0)
-            step(n - 5, affine, 1, "S")
-            step(n - 1, add_residual, 1)
-            step(n - 6, group_normed, 1, nc.vector)
-            step(n - 8, rectify, 0, "S")
+            step(n - 5, turn_normed, 1)
             if n == 3:
-                spread_bias()
-            step(n - 8, rectify, 1, "V")
-            if n + 3 >= 1:
-                step(n + 3, turn_tokens)
-            step(n - 6, quantise_normed)
-            if n + 1 >= 1:
-                step(n + 1, quantise_tokens)
-            if n == 1:
                 spread_ln()
-            step(n - 5, group_normed, 0, nc.vector)
-            for j in range(max(0, 8 * (n)), min(8, 8 * (n + 1))):
+            step(n - 6, quantise_normed)
+            if n + 2 >= 1:
+                step(n + 2, quantise_tokens)
+            if n + 4 >= 1:
+                step(n + 4, turn_tokens)
+            for j in range(max(0, 4 * (n - 5)), min(8, 4 * (n - 5 + 1))):
                 turn_ff1(j)
-            for j in range(max(0, 8 * (n)), min(8, 8 * (n + 1))):
-                group_ff1(j, on_scalar)
-            step(n - 4, affine, 0, "S")
+            step(n - 5, group_normed, 0, nc.gpsimd)
             if n + 3 >= 1:
                 step(n + 3, group_tokens, on_scalar)
-            step(n, project, 0)
-            if n == 0:
+            if n == 6:
                 quantise_ff1(0)
-            if n == 3:
+            if n == 7:
                 quantise_ff1(1)
+            step(n - 5, affine, 1, "M")
+            step(n - 8, rectify, 1, "S")
+            step(n - 5, group_normed, 1, nc.gpsimd)
+            step(n - 4, turn_normed, 0)
+            for j in range(max(0, 4 * (n - 5)), min(8, 4 * (n - 5 + 1))):
+                group_ff1(j, on_scalar)
+            step(n - 8, rectify, 0, "S")
             step(n - 7, feed_forward, 1)
-            step(n, project, 1)
+            step(n - 1, add_residual, 1)
+            step(n - 7, feed_forward, 0)
             step(n - 2, normalise, nc.gpsimd)
-            step(n - 7, add_bias, 0)
+            step(n, project, 1)
+            step(n + 1, project, 0)
+            step(n - 7, add_bias, 1)
+            step(n, add_residual, 0)

@@ -79,8 +79,8 @@ def tile_temporalatt_pb_kernel(tc, ax_cat, features, wout_w, ln_g, ln_b, ff1_w, 
             nc.sync.dma_start(out=ax_raw[:, b, s], in_=ax_view[:, b, s])
 
         load_wout(0, 0)
-        load_wout(0, 2)
         load_ax_block(0)
+        load_wout(0, 2)
         load_wout(1, 0)
         load_wout(1, 2)
         load_ax_block(1)
@@ -89,12 +89,12 @@ def tile_temporalatt_pb_kernel(tc, ax_cat, features, wout_w, ln_g, ln_b, ff1_w, 
         load_ax(2)
         load_x(1)
         load_ax(3)
+        load_x(2)
+        load_x(3)
         load_ff1(0)
         load_ff1(2)
-        load_x(2)
         load_ff1(4)
         load_ff1(6)
-        load_x(3)
         nc.sync.dma_start(out=bias_all[:], in_=ff1_b.partition_broadcast(P))
 
         w1_codes = keep.tile([P, HALVES, PASSES, BANK], U32, align_bytes=64)
@@ -189,7 +189,7 @@ def tile_temporalatt_pb_kernel(tc, ax_cat, features, wout_w, ln_g, ln_b, ff1_w, 
 
         def add_residual(i, e):
             b, s = divmod(i, SEQS)
-            if e == 0:
+            if i not in r_tiles:
                 r_tiles[i] = stage.tile([P, D], F32, tag="r", bufs=6, name="r")
                 row_sums[i] = stats.tile([P, HALVES], F32, tag="sums", name="sums")
             r, sums = r_tiles[i], row_sums[i]
@@ -319,16 +319,16 @@ def tile_temporalatt_pb_kernel(tc, ax_cat, features, wout_w, ln_g, ln_b, ff1_w, 
             )
 
         w1_block(0, 0, "S")
-        w1_block(0, 1, "V")
-        w1_block(0, 3, "V")
         turn_tokens(0)
-        group_tokens(0, on_scalar)
+        w1_block(0, 1, "V")
         w1_block(0, 2, "S")
-        quantise_tokens(0)
+        w1_block(0, 3, "V")
+        w1_block(1, 1, "V")
         w1_block(1, 0, "S")
         quantise(w1_groupeds[0][:], w1_codes[:, 0], w1_scales[:, 0])
-        w1_block(1, 1, "V")
+        group_tokens(0, on_scalar)
         w1_block(1, 3, "V")
+        quantise_tokens(0)
         w1_block(1, 2, "S")
         quantise(w1_groupeds[1][:], w1_codes[:, 1], w1_scales[:, 1])
 
@@ -336,39 +336,39 @@ def tile_temporalatt_pb_kernel(tc, ax_cat, features, wout_w, ln_g, ln_b, ff1_w, 
             if 0 <= i < TOKEN_BLOCKS:
                 piece(i, *how)
 
-        for n in range(-4, 16):
-            step(n - 8, add_bias, 0)
-            step(n - 5, affine, 0, "M")
-            step(n - 2, deviation)
-            step(n - 5, turn_normed, 1)
+        for n in range(-3, 16):
+            step(n - 8, rectify, 0, "S")
+            step(n - 1, project, 0)
+            step(n - 8, rectify, 1, "S")
             if n == 3:
                 spread_ln()
-            step(n - 6, quantise_normed)
-            if n + 2 >= 1:
-                step(n + 2, quantise_tokens)
-            if n + 4 >= 1:
-                step(n + 4, turn_tokens)
-            for j in range(max(0, 4 * (n - 5)), min(8, 4 * (n - 5 + 1))):
-                turn_ff1(j)
-            step(n - 5, group_normed, 0, nc.gpsimd)
-            if n + 3 >= 1:
-                step(n + 3, group_tokens, on_scalar)
+            step(n - 7, add_bias, 0)
+            step(n - 4, affine, 1, "S")
+            step(n - 4, group_normed, 1, nc.gpsimd)
             if n == 6:
                 quantise_ff1(0)
-            if n == 7:
+            if n == 6:
                 quantise_ff1(1)
-            step(n - 5, affine, 1, "M")
-            step(n - 8, rectify, 1, "S")
-            step(n - 5, group_normed, 1, nc.gpsimd)
-            step(n - 4, turn_normed, 0)
-            for j in range(max(0, 4 * (n - 5)), min(8, 4 * (n - 5 + 1))):
-                group_ff1(j, on_scalar)
-            step(n - 8, rectify, 0, "S")
-            step(n - 7, feed_forward, 1)
-            step(n - 1, add_residual, 1)
-            step(n - 7, feed_forward, 0)
-            step(n - 2, normalise, nc.gpsimd)
-            step(n, project, 1)
-            step(n + 1, project, 0)
             step(n - 7, add_bias, 1)
-            step(n, add_residual, 0)
+            step(n - 4, affine, 0, "V")
+            step(n - 4, group_normed, 0, nc.gpsimd)
+            step(n - 2, deviation)
+            for j in range(max(0, 8 * (n - 5)), min(8, 8 * (n - 5 + 1))):
+                turn_ff1(j)
+            step(n - 5, quantise_normed)
+            step(n - 1, add_residual, 1)
+            if n + 2 >= 1:
+                step(n + 2, quantise_tokens)
+            step(n - 2, normalise, nc.gpsimd)
+            if n + 3 >= 1:
+                step(n + 3, turn_tokens)
+            step(n - 6, feed_forward, 0)
+            step(n - 3, turn_normed, 1)
+            step(n - 6, feed_forward, 1)
+            step(n - 1, add_residual, 0)
+            step(n - 3, turn_normed, 0)
+            if n + 3 >= 1:
+                step(n + 3, group_tokens, on_scalar)
+            step(n, project, 1)
+            for j in range(max(0, 8 * (n - 5)), min(8, 8 * (n - 5 + 1))):
+                group_ff1(j, on_scalar)

@@ -40,7 +40,7 @@ def tile_temporalatt_pb_kernel(tc, ax_cat, features, wout_w, ln_g, ln_b, ff1_w, 
         keep = stack.enter_context(tc.tile_pool(name="keep", bufs=1))
         stage = stack.enter_context(tc.tile_pool(name="stage", bufs=2))
         stats = stack.enter_context(tc.tile_pool(name="stats", bufs=4))
-        results = stack.enter_context(tc.tile_pool(name="results", bufs=3))
+        results = stack.enter_context(tc.tile_pool(name="results", bufs=4))
         psum_t = stack.enter_context(tc.psum_pool(name="psum_t", bufs=4))
         psum_mm = stack.enter_context(tc.psum_pool(name="psum_mm", bufs=4))
 
@@ -52,7 +52,7 @@ def tile_temporalatt_pb_kernel(tc, ax_cat, features, wout_w, ln_g, ln_b, ff1_w, 
         eps_col = keep.tile([P, 1], F32)
         nc.vector.memset(eps_col[:], EPS)
         warm = keep.tile([P, 1], F32)
-        nc.scalar.activation(out=warm[:], in_=eps_col[:], func=ACT.Sqrt)
+        nc.scalar.activation(out=warm[:], in_=eps_col[:], func=ACT.Abs_reciprocal_sqrt)
 
         nc.scalar.dma_start(out=ln_rows[0:2, :], in_=ln_g.rearrange("(g w) -> g w", g=PASSES))
         nc.scalar.dma_start(out=ln_rows[2:4, :], in_=ln_b.rearrange("(g w) -> g w", g=PASSES))
@@ -85,16 +85,16 @@ def tile_temporalatt_pb_kernel(tc, ax_cat, features, wout_w, ln_g, ln_b, ff1_w, 
         load_wout(1, 2)
         load_ax_block(1)
         load_ax(1)
-        load_x(0)
         load_ax(2)
-        load_x(1)
+        load_x(0)
         load_ax(3)
-        load_x(2)
-        load_x(3)
         load_ff1(0)
         load_ff1(2)
+        load_x(1)
         load_ff1(4)
+        load_x(2)
         load_ff1(6)
+        load_x(3)
         nc.sync.dma_start(out=bias_all[:], in_=ff1_b.partition_broadcast(P))
 
         w1_codes = keep.tile([P, HALVES, PASSES, BANK], U32, align_bytes=64)
@@ -161,7 +161,7 @@ def tile_temporalatt_pb_kernel(tc, ax_cat, features, wout_w, ln_g, ln_b, ff1_w, 
             banks["a", i] = turn_rows(ax_raw[:, b, s, :])
 
         def group_tokens(i, copy):
-            a_grouped = stage.tile([P, PASSES, P, PACK], BF16, align_bytes=64, tag="a_grouped", bufs=3)
+            a_grouped = stage.tile([P, PASSES, P, PACK], BF16, align_bytes=64, tag="a_grouped", bufs=5)
             group_rows(copy, banks["a", i], a_grouped[:])
             a_groupeds[i] = a_grouped
 
@@ -190,7 +190,7 @@ def tile_temporalatt_pb_kernel(tc, ax_cat, features, wout_w, ln_g, ln_b, ff1_w, 
         def add_residual(i, e):
             b, s = divmod(i, SEQS)
             if i not in r_tiles:
-                r_tiles[i] = stage.tile([P, D], F32, tag="r", bufs=6, name="r")
+                r_tiles[i] = stage.tile([P, D], F32, tag="r", bufs=7, name="r")
                 row_sums[i] = stats.tile([P, HALVES], F32, tag="sums", name="sums")
             r, sums = r_tiles[i], row_sums[i]
             x_ordered = x_raw[:, b, s, :].rearrange("p (g q t) -> p g t q", g=PASSES, t=PACK)
@@ -217,19 +217,17 @@ def tile_temporalatt_pb_kernel(tc, ax_cat, features, wout_w, ln_g, ln_b, ff1_w, 
                 out=squares[:], in_=r_tiles[i][:], func=ACT.Square, bias=neg_mean[:], accum_out=sum_sq[:]
             )
             std = stats.tile([P, 1], F32, tag="std")
-            nc.scalar.activation(out=std[:], in_=sum_sq[:], func=ACT.Sqrt, scale=1.0 / D, bias=eps_col[:])
+            nc.scalar.activation(out=std[:], in_=sum_sq[:], func=ACT.Abs_reciprocal_sqrt, scale=1.0 / D, bias=eps_col[:])
             neg_means[i] = neg_mean
             stds[i] = std
 
         def normalise(i, engine):
-            inv_std = stats.tile([P, 1], F32, tag="inv_std")
-            nc.vector.reciprocal(out=inv_std[:], in_=stds[i][:])
-            z = stage.tile([P, D], F32, tag="z", bufs=3)
+            z = stage.tile([P, D], F32, tag="z", bufs=4)
             engine.tensor_scalar(
                 out=z[:],
                 in0=r_tiles[i][:],
                 scalar1=neg_means[i][:],
-                scalar2=inv_std[:],
+                scalar2=stds[i][:],
                 op0=ALU.add,
                 op1=ALU.mult,
             )
@@ -245,7 +243,7 @@ def tile_temporalatt_pb_kernel(tc, ax_cat, features, wout_w, ln_g, ln_b, ff1_w, 
 
         def affine(i, g, engine):
             if (i,) not in plane_tiles:
-                plane_tiles[i,] = stage.tile([P, PASSES, PACK, P], BF16, tag="planes", bufs=2, name="planes")
+                plane_tiles[i,] = stage.tile([P, PASSES, PACK, P], BF16, tag="planes", bufs=3, name="planes")
             planes = plane_tiles[i,]
             for t in range(PACK):
                 j = PACK * g + t
@@ -264,7 +262,7 @@ def tile_temporalatt_pb_kernel(tc, ax_cat, features, wout_w, ln_g, ln_b, ff1_w, 
         def group_normed(i, g, engine):
             if i not in m_groupeds:
                 m_groupeds[i] = stage.tile(
-                    [P, PASSES, P, PACK], BF16, align_bytes=64, tag="m_grouped", bufs=2, name="m_grouped"
+                    [P, PASSES, P, PACK], BF16, align_bytes=64, tag="m_grouped", bufs=3, name="m_grouped"
                 )
             out, in_ = m_groupeds[i][:, g], plane_tiles[i,][:, g].rearrange("p t r -> p r t")
             if engine is nc.gpsimd:
@@ -278,25 +276,32 @@ def tile_temporalatt_pb_kernel(tc, ax_cat, features, wout_w, ln_g, ln_b, ff1_w, 
         def feed_forward(i, h):
             o_banks[i, h] = matmul_group(m_codes[:, i], m_scales[:, i], w2_codes[:, h], w2_scales[:, h])
 
+        def bank_pieces(i, h):
+            pieces = 2 if i == TOKEN_BLOCKS - 1 else 1
+            width = BANK // pieces
+            return [(k * width, (k + 1) * width) for k in range(pieces)]
+
         def add_bias(i, h):
             if i not in results_of:
                 results_of[i] = results.tile([P, D], F32, tag="result", name="result")
-            cols = slice(h * BANK, (h + 1) * BANK)
-            nc.vector.tensor_tensor(
-                out=results_of[i][:, cols], in0=o_banks[i, h][:], in1=bias_all[:, cols], op=ALU.add
-            )
+            for lo, hi in bank_pieces(i, h):
+                cols = slice(h * BANK + lo, h * BANK + hi)
+                nc.vector.tensor_tensor(
+                    out=results_of[i][:, cols], in0=o_banks[i, h][:, lo:hi], in1=bias_all[:, cols], op=ALU.add
+                )
 
         def rectify(i, h, eng):
             b, s = divmod(i, SEQS)
-            cols = slice(h * BANK, (h + 1) * BANK)
-            part = results_of[i][:, cols]
-            if eng == "V":
-                nc.vector.tensor_scalar_max(part, part, 0.0)
-            elif eng == "G":
-                nc.gpsimd.tensor_scalar(out=part, in0=part, scalar1=0.0, scalar2=0.0, op0=ALU.max, op1=ALU.add)
-            else:
-                nc.scalar.activation(out=part, in_=part, func=ACT.Relu)
-            nc.sync.dma_start(out=out_view[:, b, s, cols], in_=part)
+            for lo, hi in bank_pieces(i, h):
+                cols = slice(h * BANK + lo, h * BANK + hi)
+                part = results_of[i][:, cols]
+                if eng == "V":
+                    nc.vector.tensor_scalar_max(part, part, 0.0)
+                elif eng == "G":
+                    nc.gpsimd.tensor_scalar(out=part, in0=part, scalar1=0.0, scalar2=0.0, op0=ALU.max, op1=ALU.add)
+                else:
+                    nc.scalar.activation(out=part, in_=part, func=ACT.Relu)
+                nc.sync.dma_start(out=out_view[:, b, s, cols], in_=part)
 
         def w1_block(e, c, eng):
             if e not in w1_groupeds:
@@ -319,56 +324,56 @@ def tile_temporalatt_pb_kernel(tc, ax_cat, features, wout_w, ln_g, ln_b, ff1_w, 
             )
 
         w1_block(0, 0, "S")
-        turn_tokens(0)
         w1_block(0, 1, "V")
         w1_block(0, 2, "S")
         w1_block(0, 3, "V")
-        w1_block(1, 1, "V")
         w1_block(1, 0, "S")
+        w1_block(1, 1, "V")
         quantise(w1_groupeds[0][:], w1_codes[:, 0], w1_scales[:, 0])
+        turn_tokens(0)
         group_tokens(0, on_scalar)
+        w1_block(1, 2, "S")
         w1_block(1, 3, "V")
         quantise_tokens(0)
-        w1_block(1, 2, "S")
         quantise(w1_groupeds[1][:], w1_codes[:, 1], w1_scales[:, 1])
 
         def step(i, piece, *how):
             if 0 <= i < TOKEN_BLOCKS:
                 piece(i, *how)
 
-        for n in range(-3, 16):
-            step(n - 8, rectify, 0, "S")
-            step(n - 1, project, 0)
-            step(n - 8, rectify, 1, "S")
-            if n == 3:
-                spread_ln()
-            step(n - 7, add_bias, 0)
-            step(n - 4, affine, 1, "S")
-            step(n - 4, group_normed, 1, nc.gpsimd)
-            if n == 6:
-                quantise_ff1(0)
-            if n == 6:
-                quantise_ff1(1)
-            step(n - 7, add_bias, 1)
-            step(n - 4, affine, 0, "V")
-            step(n - 4, group_normed, 0, nc.gpsimd)
-            step(n - 2, deviation)
-            for j in range(max(0, 8 * (n - 5)), min(8, 8 * (n - 5 + 1))):
-                turn_ff1(j)
-            step(n - 5, quantise_normed)
-            step(n - 1, add_residual, 1)
-            if n + 2 >= 1:
-                step(n + 2, quantise_tokens)
-            step(n - 2, normalise, nc.gpsimd)
-            if n + 3 >= 1:
-                step(n + 3, turn_tokens)
-            step(n - 6, feed_forward, 0)
-            step(n - 3, turn_normed, 1)
+        for n in range(-4, 15):
+            step(n - 5, group_normed, 1, nc.gpsimd)
+            step(n - 2, add_residual, 1)
             step(n - 6, feed_forward, 1)
-            step(n - 1, add_residual, 0)
-            step(n - 3, turn_normed, 0)
+            step(n - 7, rectify, 1, "S")
             if n + 3 >= 1:
                 step(n + 3, group_tokens, on_scalar)
-            step(n, project, 1)
+            step(n - 2, add_residual, 0)
+            step(n - 5, group_normed, 0, nc.gpsimd)
+            if n + 2 >= 1:
+                step(n + 2, quantise_tokens)
+            for j in range(max(0, 8 * (n - 5)), min(8, 8 * (n - 5 + 1))):
+                turn_ff1(j)
+            step(n - 4, affine, 0, "V")
+            step(n - 4, affine, 1, "S")
+            step(n - 7, rectify, 0, "S")
+            if n + 4 >= 1:
+                step(n + 4, turn_tokens)
+            step(n - 5, quantise_normed)
+            step(n - 6, feed_forward, 0)
+            if n == 2:
+                spread_ln()
+            step(n - 6, add_bias, 1)
+            step(n - 1, project, 1)
+            step(n - 6, add_bias, 0)
+            step(n - 3, normalise, nc.gpsimd)
+            step(n - 1, project, 0)
             for j in range(max(0, 8 * (n - 5)), min(8, 8 * (n - 5 + 1))):
                 group_ff1(j, on_scalar)
+            step(n - 2, deviation)
+            step(n - 3, turn_normed, 1)
+            if n == 5:
+                quantise_ff1(0)
+            if n == 5:
+                quantise_ff1(1)
+            step(n - 3, turn_normed, 0)

@@ -54,8 +54,8 @@ def tile_temporalatt_pb_kernel(tc, ax_cat, features, wout_w, ln_g, ln_b, ff1_w, 
         warm = keep.tile([P, 1], F32)
         nc.scalar.activation(out=warm[:], in_=eps_col[:], func=ACT.Abs_reciprocal_sqrt)
 
-        nc.scalar.dma_start(out=ln_rows[0:2, :], in_=ln_g.rearrange("(g w) -> g w", g=PASSES))
-        nc.scalar.dma_start(out=ln_rows[2:4, :], in_=ln_b.rearrange("(g w) -> g w", g=PASSES))
+        nc.gpsimd.dma_start(out=ln_rows[0:2, :], in_=ln_g.rearrange("(g w) -> g w", g=PASSES))
+        nc.gpsimd.dma_start(out=ln_rows[2:4, :], in_=ln_b.rearrange("(g w) -> g w", g=PASSES))
 
         wout_raw = keep.tile([P, 2, 4, D], BF16)
         ax_raw = keep.tile([P, TIME_BLOCKS, SEQS, D], BF16)
@@ -71,30 +71,31 @@ def tile_temporalatt_pb_kernel(tc, ax_cat, features, wout_w, ln_g, ln_b, ff1_w, 
         def load_ff1(j):
             nc.sync.dma_start(out=ff1_raw[:, j : j + 2], in_=ff1_view[:, j : j + 2])
 
-        def load_wout(g, t):
-            nc.sync.dma_start(out=wout_raw[:, g, t : t + 2], in_=wout_view[:, g, t : t + 2])
+        def load_wout(g, t, count):
+            nc.sync.dma_start(out=wout_raw[:, g, t : t + count], in_=wout_view[:, g, t : t + count])
 
         def load_ax_block(i):
             b, s = divmod(i, SEQS)
             nc.sync.dma_start(out=ax_raw[:, b, s], in_=ax_view[:, b, s])
 
-        load_wout(0, 0)
+        load_wout(0, 0, 2)
+        load_wout(0, 2, 2)
         load_ax_block(0)
-        load_wout(0, 2)
-        load_wout(1, 0)
-        load_wout(1, 2)
+        load_wout(1, 0, 2)
+        load_wout(1, 2, 1)
+        load_wout(1, 3, 1)
         load_ax_block(1)
         load_ax(1)
         load_ax(2)
-        load_x(0)
         load_ax(3)
+        load_x(0)
+        load_x(1)
         load_ff1(0)
         load_ff1(2)
-        load_x(1)
-        load_ff1(4)
         load_x(2)
-        load_ff1(6)
         load_x(3)
+        load_ff1(4)
+        load_ff1(6)
         nc.sync.dma_start(out=bias_all[:], in_=ff1_b.partition_broadcast(P))
 
         w1_codes = keep.tile([P, HALVES, PASSES, BANK], U32, align_bytes=64)
@@ -326,54 +327,54 @@ def tile_temporalatt_pb_kernel(tc, ax_cat, features, wout_w, ln_g, ln_b, ff1_w, 
         w1_block(0, 0, "S")
         w1_block(0, 1, "V")
         w1_block(0, 2, "S")
+        turn_tokens(0)
+        group_tokens(0, on_scalar)
         w1_block(0, 3, "V")
+        quantise_tokens(0)
         w1_block(1, 0, "S")
         w1_block(1, 1, "V")
         quantise(w1_groupeds[0][:], w1_codes[:, 0], w1_scales[:, 0])
-        turn_tokens(0)
-        group_tokens(0, on_scalar)
         w1_block(1, 2, "S")
-        w1_block(1, 3, "V")
-        quantise_tokens(0)
+        w1_block(1, 3, "S")
         quantise(w1_groupeds[1][:], w1_codes[:, 1], w1_scales[:, 1])
 
         def step(i, piece, *how):
             if 0 <= i < TOKEN_BLOCKS:
                 piece(i, *how)
 
-        for n in range(-4, 15):
-            step(n - 5, group_normed, 1, nc.gpsimd)
-            step(n - 2, add_residual, 1)
-            step(n - 6, feed_forward, 1)
-            step(n - 7, rectify, 1, "S")
-            if n + 3 >= 1:
-                step(n + 3, group_tokens, on_scalar)
-            step(n - 2, add_residual, 0)
-            step(n - 5, group_normed, 0, nc.gpsimd)
+        for n in range(-4, 16):
+            step(n - 8, add_bias, 1)
+            for j in range(max(0, 4 * (n - 5)), min(8, 4 * (n - 5 + 1))):
+                turn_ff1(j)
+            if n == 6:
+                quantise_ff1(0)
+            if n == 7:
+                quantise_ff1(1)
             if n + 2 >= 1:
                 step(n + 2, quantise_tokens)
-            for j in range(max(0, 8 * (n - 5)), min(8, 8 * (n - 5 + 1))):
-                turn_ff1(j)
-            step(n - 4, affine, 0, "V")
-            step(n - 4, affine, 1, "S")
-            step(n - 7, rectify, 0, "S")
+            if n == 1:
+                spread_ln()
             if n + 4 >= 1:
                 step(n + 4, turn_tokens)
-            step(n - 5, quantise_normed)
-            step(n - 6, feed_forward, 0)
-            if n == 2:
-                spread_ln()
-            step(n - 6, add_bias, 1)
+            step(n - 5, affine, 1, "S" if n - 5 < 7 else "V")
             step(n - 1, project, 1)
-            step(n - 6, add_bias, 0)
-            step(n - 3, normalise, nc.gpsimd)
+            step(n - 8, feed_forward, 0)
             step(n - 1, project, 0)
-            for j in range(max(0, 8 * (n - 5)), min(8, 8 * (n - 5 + 1))):
-                group_ff1(j, on_scalar)
+            step(n - 7, feed_forward, 1)
+            step(n - 2, add_residual, 1)
+            step(n - 4, turn_normed, 1)
+            step(n - 8, add_bias, 0)
+            step(n - 2, add_residual, 0)
+            step(n - 6, group_normed, 0, nc.gpsimd)
+            step(n - 8, rectify, 1, "S")
+            step(n - 5, affine, 0, ("V", "S")[(n - 5) % 2])
+            for j in range(max(0, 4 * (n - 5)), min(8, 4 * (n - 5 + 1))):
+                group_ff1(j, (on_scalar, on_vector)[j % 2])
+            step(n - 8, rectify, 0, "S")
+            step(n - 6, quantise_normed)
+            step(n - 3, normalise, nc.gpsimd if n - 3 < 7 else nc.vector)
+            step(n - 5, group_normed, 1, nc.gpsimd)
+            if n + 4 >= 1:
+                step(n + 4, group_tokens, on_scalar)
             step(n - 2, deviation)
-            step(n - 3, turn_normed, 1)
-            if n == 5:
-                quantise_ff1(0)
-            if n == 5:
-                quantise_ff1(1)
-            step(n - 3, turn_normed, 0)
+            step(n - 4, turn_normed, 0)

@@ -87,14 +87,14 @@ def tile_temporalatt_pb_kernel(tc, ax_cat, features, wout_w, ln_g, ln_b, ff1_w, 
         load_ax_block(1)
         load_ax(1)
         load_ax(2)
-        load_ax(3)
         load_x(0)
+        load_ax(3)
         load_x(1)
         load_ff1(0)
         load_ff1(2)
+        load_ff1(4)
         load_x(2)
         load_x(3)
-        load_ff1(4)
         load_ff1(6)
         nc.sync.dma_start(out=bias_all[:], in_=ff1_b.partition_broadcast(P))
 
@@ -327,15 +327,15 @@ def tile_temporalatt_pb_kernel(tc, ax_cat, features, wout_w, ln_g, ln_b, ff1_w, 
         w1_block(0, 0, "S")
         w1_block(0, 1, "V")
         w1_block(0, 2, "S")
+        w1_block(0, 3, "V")
+        quantise(w1_groupeds[0][:], w1_codes[:, 0], w1_scales[:, 0])
         turn_tokens(0)
         group_tokens(0, on_scalar)
-        w1_block(0, 3, "V")
-        quantise_tokens(0)
         w1_block(1, 0, "S")
         w1_block(1, 1, "V")
-        quantise(w1_groupeds[0][:], w1_codes[:, 0], w1_scales[:, 0])
         w1_block(1, 2, "S")
-        w1_block(1, 3, "S")
+        quantise_tokens(0)
+        w1_block(1, 3, "V")
         quantise(w1_groupeds[1][:], w1_codes[:, 1], w1_scales[:, 1])
 
         def step(i, piece, *how):
@@ -343,38 +343,38 @@ def tile_temporalatt_pb_kernel(tc, ax_cat, features, wout_w, ln_g, ln_b, ff1_w, 
                 piece(i, *how)
 
         for n in range(-4, 16):
-            step(n - 8, add_bias, 1)
+            step(n - 2, add_residual, 1)
             for j in range(max(0, 4 * (n - 5)), min(8, 4 * (n - 5 + 1))):
                 turn_ff1(j)
+            step(n - 2, add_residual, 0)
+            step(n - 8, feed_forward, 0)
+            if n + 4 >= 1:
+                step(n + 4, turn_tokens)
+            step(n - 8, add_bias, 1)
+            step(n - 8, add_bias, 0)
+            step(n - 1, project, 1)
             if n == 6:
                 quantise_ff1(0)
             if n == 7:
                 quantise_ff1(1)
-            if n + 2 >= 1:
-                step(n + 2, quantise_tokens)
-            if n == 1:
+            step(n - 5, affine, 1, "S")
+            if n == 0:
                 spread_ln()
-            if n + 4 >= 1:
-                step(n + 4, turn_tokens)
-            step(n - 5, affine, 1, "S" if n - 5 < 7 else "V")
-            step(n - 1, project, 1)
-            step(n - 8, feed_forward, 0)
-            step(n - 1, project, 0)
-            step(n - 7, feed_forward, 1)
-            step(n - 2, add_residual, 1)
-            step(n - 4, turn_normed, 1)
-            step(n - 8, add_bias, 0)
-            step(n - 2, add_residual, 0)
-            step(n - 6, group_normed, 0, nc.gpsimd)
-            step(n - 8, rectify, 1, "S")
             step(n - 5, affine, 0, ("V", "S")[(n - 5) % 2])
-            for j in range(max(0, 4 * (n - 5)), min(8, 4 * (n - 5 + 1))):
-                group_ff1(j, (on_scalar, on_vector)[j % 2])
-            step(n - 8, rectify, 0, "S")
-            step(n - 6, quantise_normed)
-            step(n - 3, normalise, nc.gpsimd if n - 3 < 7 else nc.vector)
-            step(n - 5, group_normed, 1, nc.gpsimd)
             if n + 4 >= 1:
                 step(n + 4, group_tokens, on_scalar)
             step(n - 2, deviation)
+            step(n - 6, group_normed, 0, nc.gpsimd)
+            step(n - 5, group_normed, 1, nc.gpsimd)
+            if n + 2 >= 1:
+                step(n + 2, quantise_tokens)
+            step(n - 1, project, 0)
+            step(n - 4, turn_normed, 1)
             step(n - 4, turn_normed, 0)
+            step(n - 8, rectify, 1, "S")
+            step(n - 6, quantise_normed)
+            step(n - 8, rectify, 0, "S")
+            step(n - 7, feed_forward, 1)
+            for j in range(max(0, 4 * (n - 5)), min(8, 4 * (n - 5 + 1))):
+                group_ff1(j, (on_scalar, on_vector)[j % 2])
+            step(n - 3, normalise, nc.gpsimd if n - 3 < 6 else nc.vector)

@@ -78,9 +78,9 @@ def tile_temporalatt_pb_kernel(tc, ax_cat, features, wout_w, ln_g, ln_b, ff1_w, 
             b, s = divmod(i, SEQS)
             nc.sync.dma_start(out=ax_raw[:, b, s], in_=ax_view[:, b, s])
 
+        load_ax_block(0)
         load_wout(0, 0, 2)
         load_wout(0, 2, 2)
-        load_ax_block(0)
         load_wout(1, 0, 2)
         load_wout(1, 2, 1)
         load_wout(1, 3, 1)
@@ -89,13 +89,13 @@ def tile_temporalatt_pb_kernel(tc, ax_cat, features, wout_w, ln_g, ln_b, ff1_w, 
         load_ax(2)
         load_x(0)
         load_ax(3)
-        load_x(1)
         load_ff1(0)
         load_ff1(2)
+        load_x(1)
         load_ff1(4)
+        load_ff1(6)
         load_x(2)
         load_x(3)
-        load_ff1(6)
         nc.sync.dma_start(out=bias_all[:], in_=ff1_b.partition_broadcast(P))
 
         w1_codes = keep.tile([P, HALVES, PASSES, BANK], U32, align_bytes=64)
@@ -324,18 +324,18 @@ def tile_temporalatt_pb_kernel(tc, ax_cat, features, wout_w, ln_g, ln_b, ff1_w, 
                 in_=ln_bank[:, 0:2, 0:4].bitcast(BF16).rearrange("p u (r e) -> p u r e", e=2),
             )
 
-        w1_block(0, 0, "S")
-        w1_block(0, 1, "V")
-        w1_block(0, 2, "S")
-        w1_block(0, 3, "V")
-        quantise(w1_groupeds[0][:], w1_codes[:, 0], w1_scales[:, 0])
         turn_tokens(0)
         group_tokens(0, on_scalar)
-        w1_block(1, 0, "S")
-        w1_block(1, 1, "V")
-        w1_block(1, 2, "S")
+        w1_block(0, 0, "V")
+        w1_block(0, 1, "S")
         quantise_tokens(0)
-        w1_block(1, 3, "V")
+        w1_block(0, 2, "V")
+        w1_block(0, 3, "S")
+        w1_block(1, 0, "V")
+        w1_block(1, 1, "S")
+        quantise(w1_groupeds[0][:], w1_codes[:, 0], w1_scales[:, 0])
+        w1_block(1, 2, "V")
+        w1_block(1, 3, "S")
         quantise(w1_groupeds[1][:], w1_codes[:, 1], w1_scales[:, 1])
 
         def step(i, piece, *how):
@@ -343,38 +343,38 @@ def tile_temporalatt_pb_kernel(tc, ax_cat, features, wout_w, ln_g, ln_b, ff1_w, 
                 piece(i, *how)
 
         for n in range(-4, 16):
-            step(n - 2, add_residual, 1)
-            for j in range(max(0, 4 * (n - 5)), min(8, 4 * (n - 5 + 1))):
-                turn_ff1(j)
-            step(n - 2, add_residual, 0)
-            step(n - 8, feed_forward, 0)
-            if n + 4 >= 1:
-                step(n + 4, turn_tokens)
-            step(n - 8, add_bias, 1)
-            step(n - 8, add_bias, 0)
-            step(n - 1, project, 1)
-            if n == 6:
+            if n == 5:
                 quantise_ff1(0)
             if n == 7:
                 quantise_ff1(1)
-            step(n - 5, affine, 1, "S")
-            if n == 0:
-                spread_ln()
-            step(n - 5, affine, 0, ("V", "S")[(n - 5) % 2])
-            if n + 4 >= 1:
-                step(n + 4, group_tokens, on_scalar)
-            step(n - 2, deviation)
-            step(n - 6, group_normed, 0, nc.gpsimd)
-            step(n - 5, group_normed, 1, nc.gpsimd)
             if n + 2 >= 1:
                 step(n + 2, quantise_tokens)
-            step(n - 1, project, 0)
-            step(n - 4, turn_normed, 1)
+            step(n - 2, project, 0)
+            step(n - 2, project, 1)
+            step(n - 5, turn_normed, 1)
+            for j in range(max(0, 6 * (n - 4)), min(8, 6 * (n - 4 + 1))):
+                turn_ff1(j)
             step(n - 4, turn_normed, 0)
-            step(n - 8, rectify, 1, "S")
-            step(n - 6, quantise_normed)
-            step(n - 8, rectify, 0, "S")
-            step(n - 7, feed_forward, 1)
-            for j in range(max(0, 4 * (n - 5)), min(8, 4 * (n - 5 + 1))):
+            step(n - 8, add_bias, 0)
+            if n + 3 >= 1:
+                step(n + 3, group_tokens, on_scalar)
+            step(n - 2, add_residual, 0)
+            step(n - 2, add_residual, 1)
+            step(n - 8, add_bias, 1)
+            step(n - 3, normalise, nc.vector)
+            step(n - 6, group_normed, 1, nc.gpsimd)
+            step(n - 5, affine, 1, "S" if n - 5 < 5 else "V")
+            for j in range(max(0, 6 * (n - 4)), min(8, 6 * (n - 4 + 1))):
                 group_ff1(j, (on_scalar, on_vector)[j % 2])
-            step(n - 3, normalise, nc.gpsimd if n - 3 < 6 else nc.vector)
+            if n == 2:
+                spread_ln()
+            step(n - 5, group_normed, 0, nc.gpsimd)
+            step(n - 2, deviation)
+            if n + 4 >= 1:
+                step(n + 4, turn_tokens)
+            step(n - 4, affine, 0, "S")
+            step(n - 8, rectify, 0, "S")
+            step(n - 6, quantise_normed)
+            step(n - 7, feed_forward, 0)
+            step(n - 8, rectify, 1, "S")
+            step(n - 7, feed_forward, 1)

from contextlib import ExitStack

import concourse.mybir as mybir
from concourse.masks import make_identity

F32 = mybir.dt.float32
BF16 = mybir.dt.bfloat16
U32 = mybir.dt.uint32
U8 = mybir.dt.uint8
FP8X4 = mybir.dt.float8_e4m3fn_x4
ACT = mybir.ActivationFunctionType
ALU = mybir.AluOpType

P = 128
PACK = 4
D = 1024
PASSES = D // (P * PACK)
BANK = 512
HALVES = D // BANK
ROW_BLOCKS = D // P
SEQS = 2
TIME_BLOCKS = 4
TOKEN_BLOCKS = SEQS * TIME_BLOCKS
EPS = 1e-5

FLOPS = 2 * 2 * (SEQS * 512) * D * D


def tile_temporalatt_pb_kernel(tc, ax_cat, features, wout_w, ln_g, ln_b, ff1_w, ff1_b, out):
    nc = tc.nc

    ax_view = ax_cat.rearrange("s (b p) k -> p b s k", p=P)
    x_view = features.rearrange("o (b p) s d -> p (o b) s d", p=P)
    out_view = out.rearrange("s (b p) f -> p b s f", p=P)
    wout_view = wout_w.rearrange("(g p t) k -> p g t k", p=P, t=PACK)
    ff1_view = ff1_w.rearrange("(j p) k -> p j k", p=P)

    with ExitStack() as stack:
        stack.enter_context(tc.manual_schedule())
        keep = stack.enter_context(tc.tile_pool(name="keep", bufs=1))
        stage = stack.enter_context(tc.tile_pool(name="stage", bufs=2))
        stats = stack.enter_context(tc.tile_pool(name="stats", bufs=4))
        results = stack.enter_context(tc.tile_pool(name="results", bufs=4))
        psum_t = stack.enter_context(tc.psum_pool(name="psum_t", bufs=4))
        psum_mm = stack.enter_context(tc.psum_pool(name="psum_mm", bufs=4))

        ident = keep.tile([P, P], F32)
        make_identity(nc, ident[:])
        bias_all = keep.tile([P, D], BF16)
        ln_rows = keep.tile([P, BANK], BF16)
        nc.gpsimd.memset(ln_rows[:], 0.0)
        eps_col = keep.tile([P, 1], F32)
        nc.vector.memset(eps_col[:], EPS)
        warm = keep.tile([P, 1], F32)
        nc.scalar.activation(out=warm[:], in_=eps_col[:], func=ACT.Abs_reciprocal_sqrt)

        nc.gpsimd.dma_start(out=ln_rows[0:2, :], in_=ln_g.rearrange("(g w) -> g w", g=PASSES))
        nc.gpsimd.dma_start(out=ln_rows[2:4, :], in_=ln_b.rearrange("(g w) -> g w", g=PASSES))

        wout_raw = keep.tile([P, 2, 4, D], BF16)
        ax_raw = keep.tile([P, TIME_BLOCKS, SEQS, D], BF16)
        x_raw = keep.tile([P, TIME_BLOCKS, SEQS, D], BF16)
        ff1_raw = keep.tile([P, ROW_BLOCKS, D], BF16)

        def load_ax(b):
            nc.sync.dma_start(out=ax_raw[:, b], in_=ax_view[:, b])

        def load_x(b):
            nc.sync.dma_start(out=x_raw[:, b], in_=x_view[:, b])

        def load_ff1(j):
            nc.sync.dma_start(out=ff1_raw[:, j : j + 2], in_=ff1_view[:, j : j + 2])

        def load_wout(g, t, count):
            nc.sync.dma_start(out=wout_raw[:, g, t : t + count], in_=wout_view[:, g, t : t + count])

        def load_ax_block(i):
            b, s = divmod(i, SEQS)
            nc.sync.dma_start(out=ax_raw[:, b, s], in_=ax_view[:, b, s])

        load_ax_block(0)
        load_wout(0, 0, 2)
        load_wout(0, 2, 2)
        load_wout(1, 0, 2)
        load_wout(1, 2, 1)
        load_wout(1, 3, 1)
        load_ax_block(1)
        load_ax(1)
        load_ax(2)
        load_x(0)
        load_ax(3)
        load_ff1(0)
        load_ff1(2)
        load_x(1)
        load_ff1(4)
        load_ff1(6)
        load_x(2)
        load_x(3)
        nc.sync.dma_start(out=bias_all[:], in_=ff1_b.partition_broadcast(P))

        w1_codes = keep.tile([P, HALVES, PASSES, BANK], U32, align_bytes=64)
        w1_scales = keep.tile([P, HALVES, PASSES, BANK], U8, align_bytes=64)
        w2_codes = keep.tile([P, HALVES, PASSES, BANK], U32, align_bytes=64)
        w2_scales = keep.tile([P, HALVES, PASSES, BANK], U8, align_bytes=64)
        a_codes = keep.tile([P, TOKEN_BLOCKS, PASSES, P], U32, align_bytes=64)
        a_scales = keep.tile([P, TOKEN_BLOCKS, PASSES, P], U8, align_bytes=64)
        m_codes = keep.tile([P, TOKEN_BLOCKS, PASSES, P], U32, align_bytes=64)
        m_scales = keep.tile([P, TOKEN_BLOCKS, PASSES, P], U8, align_bytes=64)

        def turn_rows(raw_rows):
            words = raw_rows.bitcast(F32)
            bank = psum_t.tile([P, 4, P], F32, tag="turned")
            for g in range(PASSES):
                for u in range(2):
                    pair = words[:, 2 * P * g + u : 2 * P * (g + 1) : 2]
                    nc.tensor.transpose(bank[:, 2 * g + u, :], pair, ident[:])
            return bank

        def group_rows(copy, bank, grouped_rows):
            copy(out=grouped_rows.bitcast(F32), in_=bank[:].rearrange("p (g u) r -> p g r u", u=2))

        def quantise(grouped, codes, scales):
            nc.vector.quantize_mx(
                out=codes.rearrange("p g r -> p (g r)").bitcast(FP8X4),
                scales=scales.rearrange("p g r -> p (g r)"),
                in_=grouped.rearrange("p g r t -> p (g r t)"),
            )

        def matmul_group(lhs_codes, lhs_scales, rhs_codes, rhs_scales):
            acc = psum_mm.tile([P, BANK], F32, tag="acc")
            for g in range(PASSES):
                nc.tensor.matmul_mx(
                    out=acc[:],
                    lhsT=lhs_codes[:, g, :].bitcast(FP8X4),
                    lhsT_scale=lhs_scales[:, g, :],
                    rhs=rhs_codes[:, g, :].bitcast(FP8X4),
                    rhs_scale=rhs_scales[:, g, :],
                    start=(g == 0),
                    stop=(g == PASSES - 1),
                )
            return acc

        on_scalar, on_vector = nc.scalar.copy, nc.vector.tensor_copy

        a_groupeds = {}
        w2_groupeds = {}
        y_banks = {}
        r_tiles = {}
        row_sums = {}
        neg_means = {}
        stds = {}
        z_tiles = {}
        zt_banks = {}
        plane_tiles = {}
        m_groupeds = {}
        o_banks = {}
        results_of = {}
        banks = {}

        def turn_tokens(i):
            b, s = divmod(i, SEQS)
            banks["a", i] = turn_rows(ax_raw[:, b, s, :])

        def group_tokens(i, copy):
            a_grouped = stage.tile([P, PASSES, P, PACK], BF16, align_bytes=64, tag="a_grouped", bufs=5)
            group_rows(copy, banks["a", i], a_grouped[:])
            a_groupeds[i] = a_grouped

        def quantise_tokens(i):
            quantise(a_groupeds[i][:], a_codes[:, i], a_scales[:, i])

        def new_w_grouped():
            w_grouped = stage.tile([P, PASSES, BANK, PACK], BF16, align_bytes=64, tag="w_grouped")
            return w_grouped

        def turn_ff1(j):
            banks["w", j] = turn_rows(ff1_raw[:, j, :])

        def group_ff1(j, copy):
            h, c = divmod(j, 4)
            if c == 0:
                w2_groupeds[h] = new_w_grouped()
            group_rows(copy, banks["w", j], w2_groupeds[h][:, :, c * P : (c + 1) * P, :])

        def quantise_ff1(h):
            quantise(w2_groupeds[h][:], w2_codes[:, h], w2_scales[:, h])

        def project(i, e):
            y_banks[i, e] = matmul_group(a_codes[:, i], a_scales[:, i], w1_codes[:, e], w1_scales[:, e])

        def add_residual(i, e):
            b, s = divmod(i, SEQS)
            if i not in r_tiles:
                r_tiles[i] = stage.tile([P, D], F32, tag="r", bufs=7, name="r")
                row_sums[i] = stats.tile([P, HALVES], F32, tag="sums", name="sums")
            r, sums = r_tiles[i], row_sums[i]
            x_ordered = x_raw[:, b, s, :].rearrange("p (g q t) -> p g t q", g=PASSES, t=PACK)
            if True:
                nc.vector.scalar_tensor_tensor(
                    out=r[:, e * BANK : (e + 1) * BANK].rearrange("p (t q) -> p t q", t=PACK),
                    in0=y_banks[i, e][:].rearrange("p (t q) -> p t q", t=PACK),
                    scalar=1.0,
                    in1=x_ordered[:, e],
                    op0=ALU.mult,
                    op1=ALU.add,
                    accum_out=sums[:, e : e + 1],
                )

        def deviation(i):
            scaled = stats.tile([P, HALVES], F32, tag="scaled")
            neg_mean = stats.tile([P, 1], F32, tag="neg_mean")
            nc.scalar.activation(
                out=scaled[:], in_=row_sums[i][:], func=ACT.Identity, scale=-1.0 / D, accum_out=neg_mean[:]
            )
            squares = stage.tile([P, D], BF16, tag="squares")
            sum_sq = stats.tile([P, 1], F32, tag="sum_sq")
            nc.scalar.activation(
                out=squares[:], in_=r_tiles[i][:], func=ACT.Square, bias=neg_mean[:], accum_out=sum_sq[:]
            )
            std = stats.tile([P, 1], F32, tag="std")
            nc.scalar.activation(out=std[:], in_=sum_sq[:], func=ACT.Abs_reciprocal_sqrt, scale=1.0 / D, bias=eps_col[:])
            neg_means[i] = neg_mean
            stds[i] = std

        def normalise(i, engine):
            z = stage.tile([P, D], F32, tag="z", bufs=4)
            engine.tensor_scalar(
                out=z[:],
                in0=r_tiles[i][:],
                scalar1=neg_means[i][:],
                scalar2=stds[i][:],
                op0=ALU.add,
                op1=ALU.mult,
            )
            z_tiles[i] = z

        def turn_normed(i, g):
            if True:
                bank = psum_t.tile([P, PACK, P], F32, tag="turned")
                for t in range(PACK):
                    first = g * BANK + t * P
                    nc.tensor.transpose(bank[:, t, :], z_tiles[i][:, first : first + P], ident[:])
                zt_banks[i, g] = bank

        def affine(i, g, engine):
            if (i,) not in plane_tiles:
                plane_tiles[i,] = stage.tile([P, PASSES, PACK, P], BF16, tag="planes", bufs=3, name="planes")
            planes = plane_tiles[i,]
            for t in range(PACK):
                j = PACK * g + t
                if engine == "V" or (engine == "M" and t % 2):
                    nc.vector.tensor_scalar(out=planes[:, g, t, :], in0=zt_banks[i, g][:, t, :], scalar1=gain_shift[:, j : j + 1],
                        scalar2=gain_shift[:, ROW_BLOCKS + j : ROW_BLOCKS + j + 1], op0=ALU.mult, op1=ALU.add)
                else:
                    nc.scalar.activation(
                        out=planes[:, g, t, :],
                        in_=zt_banks[i, g][:, t, :],
                        func=ACT.Identity,
                        scale=gain_shift[:, j : j + 1],
                        bias=gain_shift[:, ROW_BLOCKS + j : ROW_BLOCKS + j + 1],
                    )

        def group_normed(i, g, engine):
            if i not in m_groupeds:
                m_groupeds[i] = stage.tile(
                    [P, PASSES, P, PACK], BF16, align_bytes=64, tag="m_grouped", bufs=3, name="m_grouped"
                )
            out, in_ = m_groupeds[i][:, g], plane_tiles[i,][:, g].rearrange("p t r -> p r t")
            if engine is nc.gpsimd:
                engine.tensor_scalar(out=out, in0=in_, scalar1=1.0, scalar2=0.0, op0=ALU.mult, op1=ALU.add)
            else:
                engine.tensor_copy(out=out, in_=in_)

        def quantise_normed(i):
            quantise(m_groupeds[i][:], m_codes[:, i], m_scales[:, i])

        def feed_forward(i, h):
            o_banks[i, h] = matmul_group(m_codes[:, i], m_scales[:, i], w2_codes[:, h], w2_scales[:, h])

        def bank_pieces(i, h):
            pieces = 2 if i == TOKEN_BLOCKS - 1 else 1
            width = BANK // pieces
            return [(k * width, (k + 1) * width) for k in range(pieces)]

        def add_bias(i, h):
            if i not in results_of:
                results_of[i] = results.tile([P, D], F32, tag="result", name="result")
            for lo, hi in bank_pieces(i, h):
                cols = slice(h * BANK + lo, h * BANK + hi)
                nc.vector.tensor_tensor(
                    out=results_of[i][:, cols], in0=o_banks[i, h][:, lo:hi], in1=bias_all[:, cols], op=ALU.add
                )

        def rectify(i, h, eng):
            b, s = divmod(i, SEQS)
            for lo, hi in bank_pieces(i, h):
                cols = slice(h * BANK + lo, h * BANK + hi)
                part = results_of[i][:, cols]
                if eng == "V":
                    nc.vector.tensor_scalar_max(part, part, 0.0)
                elif eng == "G":
                    nc.gpsimd.tensor_scalar(out=part, in0=part, scalar1=0.0, scalar2=0.0, op0=ALU.max, op1=ALU.add)
                else:
                    nc.scalar.activation(out=part, in_=part, func=ACT.Relu)
                nc.sync.dma_start(out=out_view[:, b, s, cols], in_=part)

        def w1_block(e, c, eng):
            if e not in w1_groupeds:
                w1_groupeds[e] = new_w_grouped()
            banks["w1", e, c] = turn_rows(wout_raw[:, e, c, :])
            group_rows(on_scalar if eng == "S" else on_vector, banks["w1", e, c], w1_groupeds[e][:, :, c * P : (c + 1) * P, :])

        w1_groupeds = {}

        gain_shift = keep.tile([P, 2 * ROW_BLOCKS], F32)

        def spread_ln():
            ln_words = ln_rows[:].bitcast(F32)
            ln_bank = psum_t.tile([P, 4, P], F32, tag="turned")
            for u in range(2):
                nc.tensor.transpose(ln_bank[:, u, :], ln_words[:, u : 2 * P : 2], ident[:])
            nc.vector.tensor_copy(
                out=gain_shift[:].rearrange("p (r u e) -> p u r e", u=2, e=2),
                in_=ln_bank[:, 0:2, 0:4].bitcast(BF16).rearrange("p u (r e) -> p u r e", e=2),
            )

        turn_tokens(0)
        group_tokens(0, on_scalar)
        w1_block(0, 0, "V")
        w1_block(0, 1, "S")
        quantise_tokens(0)
        w1_block(0, 2, "V")
        w1_block(0, 3, "S")
        w1_block(1, 0, "V")
        w1_block(1, 1, "S")
        quantise(w1_groupeds[0][:], w1_codes[:, 0], w1_scales[:, 0])
        w1_block(1, 2, "V")
        w1_block(1, 3, "S")
        quantise(w1_groupeds[1][:], w1_codes[:, 1], w1_scales[:, 1])

        def step(i, piece, *how):
            if 0 <= i < TOKEN_BLOCKS:
                piece(i, *how)

        for n in range(-4, 16):
            if n == 5:
                quantise_ff1(0)
            if n == 7:
                quantise_ff1(1)
            if n + 2 >= 1:
                step(n + 2, quantise_tokens)
            step(n - 2, project, 0)
            step(n - 2, project, 1)
            step(n - 5, turn_normed, 1)
            for j in range(max(0, 6 * (n - 4)), min(8, 6 * (n - 4 + 1))):
                turn_ff1(j)
            step(n - 4, turn_normed, 0)
            step(n - 8, add_bias, 0)
            if n + 3 >= 1:
                step(n + 3, group_tokens, on_scalar)
            step(n - 2, add_residual, 0)
            step(n - 2, add_residual, 1)
            step(n - 8, add_bias, 1)
            step(n - 3, normalise, nc.vector)
            step(n - 6, group_normed, 1, nc.gpsimd)
            step(n - 5, affine, 1, "S" if n - 5 < 5 else "V")
            for j in range(max(0, 6 * (n - 4)), min(8, 6 * (n - 4 + 1))):
                group_ff1(j, (on_scalar, on_vector)[j % 2])
            if n == 2:
                spread_ln()
            step(n - 5, group_normed, 0, nc.gpsimd)
            step(n - 2, deviation)
            if n + 4 >= 1:
                step(n + 4, turn_tokens)
            step(n - 4, affine, 0, "S")
            step(n - 8, rectify, 0, "S")
            step(n - 6, quantise_normed)
            step(n - 7, feed_forward, 0)
            step(n - 8, rectify, 1, "S")
            step(n - 7, feed_forward, 1)
